import numpy as np
import ml_dtypes


def mxq(x, axis, fmt="e4m3"):
    dtype, down = {"e4m3": (ml_dtypes.float8_e4m3fn, 7), "e5m2": (ml_dtypes.float8_e5m2, 14)}[fmt]
    v = np.moveaxis(np.asarray(x, np.float32).astype(ml_dtypes.bfloat16).astype(np.float64), axis, -1)
    blocks = v.reshape(v.shape[:-1] + (-1, 32))
    amax = np.abs(blocks).max(-1, keepdims=True)
    byte = np.maximum(np.where(amax > 0, np.frexp(amax)[1] - 1 + 127, 0) - down, 1)
    scale = np.exp2(byte - 127.0)
    codes = (blocks / scale).astype(np.float32).astype(dtype).astype(np.float64)
    return np.moveaxis((codes * scale).reshape(v.shape), -1, axis)


WIDE = False


def mx_kscale(k):
    if not WIDE:
        return np.ones(k)
    levels = np.array([10, -10, 5, -5, 0])
    a = np.random.permutation(np.resize(levels, k // 512 * 4)).reshape(k // 512, 4)
    idx = np.arange(k)
    return np.exp2(a[idx // 512, idx % 128 // 32])


BF16 = ml_dtypes.bfloat16


def bf(x):
    return np.asarray(x, np.float32).astype(BF16)


def f64(x):
    return np.asarray(x).astype(np.float64)


BATCH, SEQ, IN_DIM, MID_DIM, OUT_DIM = 4, 128, 2048, 2048, 2048
CB = 2.0 ** -np.round(np.log2(IN_DIM) / 2)
CA = 2.0 ** -np.round(np.log2(MID_DIM) / 2)


def signs(shape):
    return np.where(np.random.standard_normal(shape) >= 0, 1.0, -1.0)


def setup_inputs():
    s, t = mx_kscale(IN_DIM), mx_kscale(MID_DIM)
    return {"x": bf(np.random.standard_normal((BATCH, SEQ, IN_DIM)) * s),
            "scaling0": bf(0.5 + np.random.uniform(size=IN_DIM)),
            "B": bf(signs((MID_DIM, IN_DIM)) * CB / s[None, :]),
            "scaling2": bf((0.5 + np.random.uniform(size=MID_DIM)) * t),
            "A": bf(signs((OUT_DIM, MID_DIM)) * CA / t[None, :]),
            "scaling4": bf(0.5 + np.random.uniform(size=OUT_DIM)),
            "bias": bf(np.random.standard_normal(OUT_DIM))}


def reference(x, scaling0, B, scaling2, A, scaling4, bias):
    h = f64(x) * f64(scaling0)
    h = mxq(h, 2, "e4m3") @ mxq(f64(B), 1, "e4m3").T
    h = h * f64(scaling2)
    h = mxq(h, 2, "e4m3") @ mxq(f64(A), 1, "e4m3").T
    return h * f64(scaling4) + f64(bias)

@@ -1,0 +1,292 @@
+from contextlib import ExitStack
+
+import concourse.mybir as mybir
+from concourse.masks import make_identity
+
+F32 = mybir.dt.float32
+BF16 = mybir.dt.bfloat16
+U32 = mybir.dt.uint32
+U8 = mybir.dt.uint8
+I32 = mybir.dt.int32
+FP8X4 = mybir.dt.float8_e4m3fn_x4
+ACT = mybir.ActivationFunctionType
+ALU = mybir.AluOpType
+
+P = 128
+D = 2048
+NB = 4
+G = 4
+ROUNDS = 16
+RAW_BUFS = 10
+FLOPS = 2 * 512 * 2048 * 2048 * 2
+
+
+def tile_doublebinarylinear_kernel(tc, x, scaling0, B, scaling2, A, scaling4, bias, out):
+    nc = tc.nc
+    with ExitStack() as ctx:
+        const = ctx.enter_context(tc.tile_pool(name="const", bufs=1))
+        rawp = ctx.enter_context(tc.tile_pool(name="raw", bufs=RAW_BUFS))
+        grpp = ctx.enter_context(tc.tile_pool(name="grp", bufs=3))
+        codp = ctx.enter_context(tc.tile_pool(name="cod", bufs=3))
+        h2p = ctx.enter_context(tc.tile_pool(name="h2", bufs=2))
+        tmpp = ctx.enter_context(tc.tile_pool(name="tmpp", bufs=2))
+        outp = ctx.enter_context(tc.tile_pool(name="outp", bufs=3))
+        tpp = ctx.enter_context(tc.psum_pool(name="tpp", bufs=4))
+        mmp = ctx.enter_context(tc.psum_pool(name="mmp", bufs=4))
+        ctx.enter_context(tc.manual_schedule())
+
+        w_dram = [B.rearrange("(c p e) k -> c p e k", p=P, e=2), A.rearrange("(c p e) k -> c p e k", p=P, e=2)]
+        out_v = out.rearrange("b s o -> s b o")
+
+        row0 = const.tile([P, D], BF16, name="row0")
+        nc.vector.memset(row0[:].bitcast(I32), 0)
+        ones = const.tile([P, P], BF16, name="ones")
+        nc.vector.memset(ones[:], 1.0)
+        ident = const.tile([P, P], F32, name="ident")
+        make_identity(nc, ident[:])
+
+        nc.sync.dma_start(out=row0[0:1, :], in_=scaling0.rearrange("(o k) -> o k", o=1))
+        x_sb = []
+        for b in range(NB):
+            xt = const.tile([P, D], BF16, name="x%d" % b)
+            nc.sync.dma_start(out=xt[:], in_=x[b])
+            x_sb.append(xt)
+        sc2raw = const.tile([P, 16], BF16, name="sc2raw")
+        with nc.allow_non_contiguous_dma(reason="one small vector, two elements to a piece"):
+            nc.scalar.dma_start(
+                out=sc2raw[:].rearrange("p (c e) -> p c e", e=2),
+                in_=scaling2.rearrange("(c p e) -> p c e", p=P, e=2),
+            )
+        sc2t = const.tile([P, 16], F32, name="sc2t")
+        sc4b = const.tile([P, D], BF16, name="sc4b")
+        biasb = const.tile([P, D], BF16, name="biasb")
+
+        raw = {}
+
+        def load_w(r):
+            w = rawp.tile([P, 2, D], BF16, name="w", tag="w")
+            nc.sync.dma_start(out=w[:], in_=w_dram[r // 8][r % 8])
+            raw[r] = w
+
+        for r in range(RAW_BUFS):
+            load_w(r)
+            if r == 7:
+                nc.sync.dma_start(out=sc4b[:], in_=scaling4.partition_broadcast(P))
+                nc.sync.dma_start(out=biasb[:], in_=bias.partition_broadcast(P))
+
+        xg = const.tile([P, G * 512 * 4], BF16, name="xg", align_bytes=64)
+        xq = const.tile([P, G * 512], U32, name="xq", align_bytes=64)
+        xsc = const.tile([P, G * 512], U8, name="xsc", align_bytes=64)
+        h2q = const.tile([P, G * 512], U32, name="h2q", align_bytes=64)
+        h2s = const.tile([P, G * 512], U8, name="h2s", align_bytes=64)
+
+        bc = []
+        for h in range(2):
+            bt = mmp.tile([P, 1024], BF16, name="bc%d" % h, tag="mm")
+            for q in range(2):
+                nc.tensor.matmul(
+                    out=bt[:, 512 * q : 512 * q + 512],
+                    lhsT=ones[:],
+                    rhs=row0[:, 1024 * h + 512 * q : 1024 * h + 512 * q + 512],
+                    start=True,
+                    stop=True,
+                )
+            bc.append(bt)
+
+        xg_f = xg[:].bitcast(F32).rearrange("p (g t u) -> p g t u", g=G, u=2)
+
+        def quant_x(b):
+            for g in range(G):
+                c0 = g * 512 + 128 * b
+                nc.vector.quantize_mx(
+                    out=xq[:, c0 : c0 + 128].bitcast(FP8X4),
+                    scales=xsc[:, c0 : c0 + 128],
+                    in_=xg[:, 4 * c0 : 4 * c0 + 512],
+                )
+
+        for b in range(NB):
+            xf = x_sb[b][:].bitcast(F32)
+            for j in range(2):
+                cols = slice(1024 * j, 1024 * j + 1024)
+                nc.vector.tensor_tensor(out=x_sb[b][:, cols], in0=x_sb[b][:, cols], in1=bc[j][:], op=ALU.mult)
+                t = tpp.tile([P, 512], F32, name="tp", tag="tp")
+                for a in range(2):
+                    for u in range(2):
+                        k0 = 256 * (2 * j + a) + 128 * u
+                        nc.tensor.transpose(
+                            out=t[:, (2 * a + u) * 128 : (2 * a + u) * 128 + 128],
+                            in_=xf[:, k0 : k0 + 128],
+                            identity=ident[:],
+                        )
+                nc.scalar.copy(
+                    out=xg_f[:, 2 * j : 2 * j + 2, 128 * b : 128 * b + 128, :],
+                    in_=t[:].rearrange("p (a u m) -> p a m u", a=2, u=2),
+                )
+            if b == 1:
+                nc.vector.tensor_copy(out=sc2t[:], in_=sc2raw[:])
+            if b >= 1:
+                quant_x(b - 1)
+
+        grp = {}
+        cod = {}
+
+        def transposes(r, engines):
+            w = raw[r]
+            wf = w[:].bitcast(F32)
+            gt = grpp.tile([P, 4096], BF16, name="grp", tag="grp", align_bytes=64)
+            gf = gt[:].bitcast(F32)
+            for k in range(4):
+                t = tpp.tile([P, 512], F32, name="tp", tag="tp")
+                for a in range(2):
+                    for u in range(2):
+                        if r < 8:
+                            e, g = k // 2, 2 * (k % 2) + a
+                        else:
+                            e, g = a, k
+                        k0 = 256 * g + 128 * u
+                        nc.tensor.transpose(
+                            out=t[:, (2 * a + u) * 128 : (2 * a + u) * 128 + 128],
+                            in_=wf[:, e, k0 : k0 + 128],
+                            identity=ident[:],
+                        )
+                if r < 8:
+                    dst = gf[:, 512 * k : 512 * k + 512].rearrange("p (a m u) -> p a m u", a=2, u=2)
+                    src = t[:].rearrange("p (a u m) -> p a m u", a=2, u=2)
+                else:
+                    dst = gf[:, 512 * k : 512 * k + 512].rearrange("p (m a u) -> p m a u", a=2, u=2)
+                    src = t[:].rearrange("p (a u m) -> p m a u", a=2, u=2)
+                if engines[k] == "s":
+                    nc.scalar.copy(out=dst, in_=src)
+                else:
+                    nc.vector.tensor_copy(out=dst, in_=src)
+            grp[r] = gt
+            if r + RAW_BUFS < ROUNDS:
+                load_w(r + RAW_BUFS)
+
+        def quantise(r):
+            gt = grp[r]
+            wq = codp.tile([P, 1024], U32, name="wq", tag="wq", align_bytes=64)
+            ws = codp.tile([P, 1024], U8, name="ws", tag="ws", align_bytes=64)
+            for h in range(2):
+                nc.vector.quantize_mx(
+                    out=wq[:, 512 * h : 512 * h + 512].bitcast(FP8X4),
+                    scales=ws[:, 512 * h : 512 * h + 512],
+                    in_=gt[:, 2048 * h : 2048 * h + 2048],
+                )
+            cod[r] = (wq, ws)
+
+        acc = {}
+        h2c = {}
+
+        def mx1(c):
+            wq, ws = cod[c]
+            for e in range(2):
+                ps = mmp.tile([P, 512], F32, name="mm", tag="mm")
+                for g in range(G):
+                    c0 = e * 512 + g * 128
+                    nc.tensor.matmul_mx(
+                        out=ps[:],
+                        lhsT=wq[:, c0 : c0 + 128].bitcast(FP8X4),
+                        lhsT_scale=ws[:, c0 : c0 + 128],
+                        rhs=xq[:, g * 512 : g * 512 + 512].bitcast(FP8X4),
+                        rhs_scale=xsc[:, g * 512 : g * 512 + 512],
+                        start=(g == 0),
+                        stop=(g == G - 1),
+                    )
+                acc[(c, e)] = ps
+
+        def post1(c):
+            if c % 2 == 0:
+                h2c[c // 2] = h2p.tile([P, 4, 512], BF16, name="h2c", tag="h2c")
+            hc = h2c[c // 2]
+            for e in range(2):
+                nc.scalar.activation(
+                    out=hc[:, 2 * (c % 2) + e, :],
+                    in_=acc[(c, e)][:],
+                    func=ACT.Copy,
+                    scale=sc2t[:, 2 * c + e : 2 * c + e + 1],
+                )
+            if c % 2 == 1:
+                g2 = c // 2
+                hg = h2p.tile([P, 2048], BF16, name="h2g", tag="h2g", align_bytes=64)
+                nc.vector.tensor_copy(
+                    out=hg[:].rearrange("p (c i t) -> p c t i", i=4, t=4),
+                    in_=hc[:].rearrange("p t (c i) -> p c t i", i=4),
+                )
+                nc.vector.quantize_mx(
+                    out=h2q[:, g2 * 512 : g2 * 512 + 512].bitcast(FP8X4),
+                    scales=h2s[:, g2 * 512 : g2 * 512 + 512],
+                    in_=hg[:],
+                )
+
+        def mx2_pass(ps_ap, cd, b, g):
+            wq, ws = cd
+            c0 = g * 512 + 128 * b
+            nc.tensor.matmul_mx(
+                out=ps_ap,
+                lhsT=h2q[:, c0 : c0 + 128].bitcast(FP8X4),
+                lhsT_scale=h2s[:, c0 : c0 + 128],
+                rhs=wq[:, g * 256 : g * 256 + 256].bitcast(FP8X4),
+                rhs_scale=ws[:, g * 256 : g * 256 + 256],
+                start=(g == 0),
+                stop=(g == G - 1),
+            )
+
+        def mx2(r):
+            cd = cod[r]
+            if r == 8:
+                tiles = []
+                for b in range(NB):
+                    ps = mmp.tile([P, 512], F32, name="mm", tag="mm")
+                    tiles.append(ps)
+                for g in range(G):
+                    for b in range(NB):
+                        mx2_pass(tiles[b][:, 0:256], cd, b, g)
+                acc[r] = tiles
+            else:
+                tiles = []
+                for h in range(2):
+                    ps = mmp.tile([P, 512], F32, name="mm", tag="mm")
+                    for bl in range(2):
+                        for g in range(G):
+                            mx2_pass(ps[:, 256 * bl : 256 * bl + 256], cd, 2 * h + bl, g)
+                    tiles.append(ps)
+                acc[r] = tiles
+
+        def post2(r):
+            cols = slice(256 * (r - 8), 256 * (r - 8) + 256)
+            tiles = acc[r]
+            tmp = tmpp.tile([P, NB, 256], F32, name="tmp", tag="tmp")
+            n = NB // len(tiles)
+            for i, ps in enumerate(tiles):
+                nc.vector.tensor_tensor(
+                    out=tmp[:, n * i : n * i + n, :],
+                    in0=ps[:, 0 : 256 * n].rearrange("p (b o) -> p b o", b=n),
+                    in1=sc4b[:, cols].unsqueeze(1).to_broadcast([P, n, 256]),
+                    op=ALU.mult,
+                )
+            ot = outp.tile([P, NB, 256], F32, name="ot", tag="ot")
+            nc.vector.tensor_tensor(
+                out=ot[:],
+                in0=tmp[:],
+                in1=biasb[:, cols].unsqueeze(1).to_broadcast([P, NB, 256]),
+                op=ALU.add,
+            )
+            nc.sync.dma_start(out=out_v[:, :, cols], in_=ot[:])
+
+        transposes(0, "ssss")
+        quant_x(NB - 1)
+        quantise(0)
+        for r in range(ROUNDS):
+            if r + 1 < ROUNDS:
+                transposes(r + 1, "svss" if r + 1 < 8 else "ssss")
+            if r < 8:
+                mx1(r)
+            else:
+                mx2(r)
+            if r + 1 < ROUNDS:
+                quantise(r + 1)
+            if r < 8:
+                post1(r)
+            else:
+                post2(r)

@@ -20,6 +20,13 @@ ROUNDS = 16
 RAW_BUFS = 10
 FLOPS = 2 * 512 * 2048 * 2048 * 2
 
+MULTS_FIRST = True
+FINE_TAIL = True
+A_BY_HALVES = False
+W0_HALVES = True
+B_ENG = "sssv"
+A_ENG = "ssss"
+
 
 def tile_doublebinarylinear_kernel(tc, x, scaling0, B, scaling2, A, scaling4, bias, out):
     nc = tc.nc
@@ -35,7 +42,8 @@ def tile_doublebinarylinear_kernel(tc, x, scaling0, B, scaling2, A, scaling4, bi
         mmp = ctx.enter_context(tc.psum_pool(name="mmp", bufs=4))
         ctx.enter_context(tc.manual_schedule())
 
-        w_dram = [B.rearrange("(c p e) k -> c p e k", p=P, e=2), A.rearrange("(c p e) k -> c p e k", p=P, e=2)]
+        a_pat = "(c e p) k -> c p e k" if A_BY_HALVES else "(c p e) k -> c p e k"
+        w_dram = [B.rearrange("(c p e) k -> c p e k", p=P, e=2), A.rearrange(a_pat, p=P, e=2)]
         out_v = out.rearrange("b s o -> s b o")
 
         row0 = const.tile([P, D], BF16, name="row0")
@@ -65,7 +73,11 @@ def tile_doublebinarylinear_kernel(tc, x, scaling0, B, scaling2, A, scaling4, bi
 
         def load_w(r):
             w = rawp.tile([P, 2, D], BF16, name="w", tag="w")
-            nc.sync.dma_start(out=w[:], in_=w_dram[r // 8][r % 8])
+            if r == 0 and W0_HALVES:
+                for e in range(2):
+                    nc.sync.dma_start(out=w[:, e, :], in_=w_dram[0][0][:, e, :])
+            else:
+                nc.sync.dma_start(out=w[:], in_=w_dram[r // 8][r % 8])
             raw[r] = w
 
         for r in range(RAW_BUFS):
@@ -122,10 +134,12 @@ def tile_doublebinarylinear_kernel(tc, x, scaling0, B, scaling2, A, scaling4, bi
                     out=xg_f[:, 2 * j : 2 * j + 2, 128 * b : 128 * b + 128, :],
                     in_=t[:].rearrange("p (a u m) -> p a m u", a=2, u=2),
                 )
-            if b == 1:
-                nc.vector.tensor_copy(out=sc2t[:], in_=sc2raw[:])
-            if b >= 1:
+            if b >= 1 and not MULTS_FIRST:
                 quant_x(b - 1)
+        nc.gpsimd.tensor_copy(out=sc2t[:], in_=sc2raw[:])
+        if MULTS_FIRST:
+            for b in range(NB - 1):
+                quant_x(b)
 
         grp = {}
         cod = {}
@@ -149,7 +163,7 @@ def tile_doublebinarylinear_kernel(tc, x, scaling0, B, scaling2, A, scaling4, bi
                             in_=wf[:, e, k0 : k0 + 128],
                             identity=ident[:],
                         )
-                if r < 8:
+                if r < 8 or A_BY_HALVES:
                     dst = gf[:, 512 * k : 512 * k + 512].rearrange("p (a m u) -> p a m u", a=2, u=2)
                     src = t[:].rearrange("p (a u m) -> p a m u", a=2, u=2)
                 else:
@@ -209,15 +223,18 @@ def tile_doublebinarylinear_kernel(tc, x, scaling0, B, scaling2, A, scaling4, bi
             if c % 2 == 1:
                 g2 = c // 2
                 hg = h2p.tile([P, 2048], BF16, name="h2g", tag="h2g", align_bytes=64)
-                nc.vector.tensor_copy(
-                    out=hg[:].rearrange("p (c i t) -> p c t i", i=4, t=4),
-                    in_=hc[:].rearrange("p t (c i) -> p c t i", i=4),
-                )
-                nc.vector.quantize_mx(
-                    out=h2q[:, g2 * 512 : g2 * 512 + 512].bitcast(FP8X4),
-                    scales=h2s[:, g2 * 512 : g2 * 512 + 512],
-                    in_=hg[:],
-                )
+                for h in range(2):
+                    nc.vector.tensor_copy(
+                        out=hg[:, 1024 * h : 1024 * h + 1024].rearrange("p (c i t) -> p c t i", i=4, t=4),
+                        in_=hc[:, :, 256 * h : 256 * h + 256].rearrange("p t (c i) -> p c t i", i=4),
+                    )
+                for h in range(2):
+                    c0 = g2 * 512 + 256 * h
+                    nc.vector.quantize_mx(
+                        out=h2q[:, c0 : c0 + 256].bitcast(FP8X4),
+                        scales=h2s[:, c0 : c0 + 256],
+                        in_=hg[:, 1024 * h : 1024 * h + 1024],
+                    )
 
         def mx2_pass(ps_ap, cd, b, g):
             wq, ws = cd
@@ -243,6 +260,14 @@ def tile_doublebinarylinear_kernel(tc, x, scaling0, B, scaling2, A, scaling4, bi
                     for b in range(NB):
                         mx2_pass(tiles[b][:, 0:256], cd, b, g)
                 acc[r] = tiles
+            elif r == ROUNDS - 1 and FINE_TAIL:
+                tiles = []
+                for b in range(NB):
+                    ps = mmp.tile([P, 512], F32, name="mm", tag="mm")
+                    for g in range(G):
+                        mx2_pass(ps[:, 0:256], cd, b, g)
+                    tiles.append(ps)
+                acc[r] = tiles
             else:
                 tiles = []
                 for h in range(2):
@@ -257,7 +282,16 @@ def tile_doublebinarylinear_kernel(tc, x, scaling0, B, scaling2, A, scaling4, bi
             cols = slice(256 * (r - 8), 256 * (r - 8) + 256)
             tiles = acc[r]
             tmp = tmpp.tile([P, NB, 256], F32, name="tmp", tag="tmp")
+            ot = outp.tile([P, NB, 256], F32, name="ot", tag="ot")
             n = NB // len(tiles)
+            if r == ROUNDS - 1 and FINE_TAIL:
+                for b in range(NB + 1):
+                    if b < NB:
+                        nc.vector.tensor_tensor(out=tmp[:, b, :], in0=tiles[b][:, 0:256], in1=sc4b[:, cols], op=ALU.mult)
+                    if b >= 1:
+                        nc.vector.tensor_tensor(out=ot[:, b - 1, :], in0=tmp[:, b - 1, :], in1=biasb[:, cols], op=ALU.add)
+                        nc.sync.dma_start(out=out[b - 1][:, cols], in_=ot[:, b - 1, :])
+                return
             for i, ps in enumerate(tiles):
                 nc.vector.tensor_tensor(
                     out=tmp[:, n * i : n * i + n, :],
@@ -265,13 +299,13 @@ def tile_doublebinarylinear_kernel(tc, x, scaling0, B, scaling2, A, scaling4, bi
                     in1=sc4b[:, cols].unsqueeze(1).to_broadcast([P, n, 256]),
                     op=ALU.mult,
                 )
-            ot = outp.tile([P, NB, 256], F32, name="ot", tag="ot")
-            nc.vector.tensor_tensor(
-                out=ot[:],
-                in0=tmp[:],
-                in1=biasb[:, cols].unsqueeze(1).to_broadcast([P, NB, 256]),
-                op=ALU.add,
-            )
+            for h in range(2):
+                nc.vector.tensor_tensor(
+                    out=ot[:, 2 * h : 2 * h + 2, :],
+                    in0=tmp[:, 2 * h : 2 * h + 2, :],
+                    in1=biasb[:, cols].unsqueeze(1).to_broadcast([P, 2, 256]),
+                    op=ALU.add,
+                )
             nc.sync.dma_start(out=out_v[:, :, cols], in_=ot[:])
 
         transposes(0, "ssss")
@@ -279,7 +313,7 @@ def tile_doublebinarylinear_kernel(tc, x, scaling0, B, scaling2, A, scaling4, bi
         quantise(0)
         for r in range(ROUNDS):
             if r + 1 < ROUNDS:
-                transposes(r + 1, "svss" if r + 1 < 8 else "ssss")
+                transposes(r + 1, B_ENG if r + 1 < 8 else A_ENG)
             if r < 8:
                 mx1(r)
             else:

@@ -22,8 +22,13 @@ FLOPS = 2 * 512 * 2048 * 2048 * 2
 
 MULTS_FIRST = True
 FINE_TAIL = True
-A_BY_HALVES = False
+A_BY_HALVES = True
 W0_HALVES = True
+ACT_PRELOAD = True
+SC2_LATE = True
+QX_PAIRS = True
+BC_SBUF = False
+POOL_ADD_FROM = 16
 B_ENG = "sssv"
 A_ENG = "ssss"
 
@@ -48,23 +53,21 @@ def tile_doublebinarylinear_kernel(tc, x, scaling0, B, scaling2, A, scaling4, bi
 
         row0 = const.tile([P, D], BF16, name="row0")
         nc.vector.memset(row0[:].bitcast(I32), 0)
+        nc.sync.dma_start(out=row0[0:1, :], in_=scaling0.rearrange("(o k) -> o k", o=1))
         ones = const.tile([P, P], BF16, name="ones")
         nc.vector.memset(ones[:], 1.0)
         ident = const.tile([P, P], F32, name="ident")
         make_identity(nc, ident[:])
+        if ACT_PRELOAD:
+            warm = const.tile([P, 1], BF16, name="warm")
+            nc.scalar.copy(out=warm[:], in_=ones[:, 0:1])
 
-        nc.sync.dma_start(out=row0[0:1, :], in_=scaling0.rearrange("(o k) -> o k", o=1))
         x_sb = []
         for b in range(NB):
             xt = const.tile([P, D], BF16, name="x%d" % b)
             nc.sync.dma_start(out=xt[:], in_=x[b])
             x_sb.append(xt)
         sc2raw = const.tile([P, 16], BF16, name="sc2raw")
-        with nc.allow_non_contiguous_dma(reason="one small vector, two elements to a piece"):
-            nc.scalar.dma_start(
-                out=sc2raw[:].rearrange("p (c e) -> p c e", e=2),
-                in_=scaling2.rearrange("(c p e) -> p c e", p=P, e=2),
-            )
         sc2t = const.tile([P, 16], F32, name="sc2t")
         sc4b = const.tile([P, D], BF16, name="sc4b")
         biasb = const.tile([P, D], BF16, name="biasb")
@@ -82,6 +85,12 @@ def tile_doublebinarylinear_kernel(tc, x, scaling0, B, scaling2, A, scaling4, bi
 
         for r in range(RAW_BUFS):
             load_w(r)
+            if r == 0:
+                with nc.allow_non_contiguous_dma(reason="one small vector, two elements to a piece"):
+                    nc.sync.dma_start(
+                        out=sc2raw[:].rearrange("p (c e) -> p c e", e=2),
+                        in_=scaling2.rearrange("(c p e) -> p c e", p=P, e=2),
+                    )
             if r == 7:
                 nc.sync.dma_start(out=sc4b[:], in_=scaling4.partition_broadcast(P))
                 nc.sync.dma_start(out=biasb[:], in_=bias.partition_broadcast(P))
@@ -103,17 +112,22 @@ def tile_doublebinarylinear_kernel(tc, x, scaling0, B, scaling2, A, scaling4, bi
                     start=True,
                     stop=True,
                 )
-            bc.append(bt)
+            if BC_SBUF:
+                bs = const.tile([P, 1024], BF16, name="bcs%d" % h)
+                nc.scalar.copy(out=bs[:], in_=bt[:])
+                bc.append(bs)
+            else:
+                bc.append(bt)
 
         xg_f = xg[:].bitcast(F32).rearrange("p (g t u) -> p g t u", g=G, u=2)
 
-        def quant_x(b):
+        def quant_x(bp):
             for g in range(G):
-                c0 = g * 512 + 128 * b
+                c0 = g * 512 + 256 * bp
                 nc.vector.quantize_mx(
-                    out=xq[:, c0 : c0 + 128].bitcast(FP8X4),
-                    scales=xsc[:, c0 : c0 + 128],
-                    in_=xg[:, 4 * c0 : 4 * c0 + 512],
+                    out=xq[:, c0 : c0 + 256].bitcast(FP8X4),
+                    scales=xsc[:, c0 : c0 + 256],
+                    in_=xg[:, 4 * c0 : 4 * c0 + 1024],
                 )
 
         for b in range(NB):
@@ -134,12 +148,8 @@ def tile_doublebinarylinear_kernel(tc, x, scaling0, B, scaling2, A, scaling4, bi
                     out=xg_f[:, 2 * j : 2 * j + 2, 128 * b : 128 * b + 128, :],
                     in_=t[:].rearrange("p (a u m) -> p a m u", a=2, u=2),
                 )
-            if b >= 1 and not MULTS_FIRST:
-                quant_x(b - 1)
         nc.gpsimd.tensor_copy(out=sc2t[:], in_=sc2raw[:])
-        if MULTS_FIRST:
-            for b in range(NB - 1):
-                quant_x(b)
+        quant_x(0)
 
         grp = {}
         cod = {}
@@ -177,17 +187,18 @@ def tile_doublebinarylinear_kernel(tc, x, scaling0, B, scaling2, A, scaling4, bi
             if r + RAW_BUFS < ROUNDS:
                 load_w(r + RAW_BUFS)
 
-        def quantise(r):
+        def quantise(r, h):
             gt = grp[r]
-            wq = codp.tile([P, 1024], U32, name="wq", tag="wq", align_bytes=64)
-            ws = codp.tile([P, 1024], U8, name="ws", tag="ws", align_bytes=64)
-            for h in range(2):
-                nc.vector.quantize_mx(
-                    out=wq[:, 512 * h : 512 * h + 512].bitcast(FP8X4),
-                    scales=ws[:, 512 * h : 512 * h + 512],
-                    in_=gt[:, 2048 * h : 2048 * h + 2048],
-                )
-            cod[r] = (wq, ws)
+            if h == 0:
+                wq = codp.tile([P, 1024], U32, name="wq", tag="wq", align_bytes=64)
+                ws = codp.tile([P, 1024], U8, name="ws", tag="ws", align_bytes=64)
+                cod[r] = (wq, ws)
+            wq, ws = cod[r]
+            nc.vector.quantize_mx(
+                out=wq[:, 512 * h : 512 * h + 512].bitcast(FP8X4),
+                scales=ws[:, 512 * h : 512 * h + 512],
+                in_=gt[:, 2048 * h : 2048 * h + 2048],
+            )
 
         acc = {}
         h2c = {}
@@ -278,49 +289,71 @@ def tile_doublebinarylinear_kernel(tc, x, scaling0, B, scaling2, A, scaling4, bi
                     tiles.append(ps)
                 acc[r] = tiles
 
-        def post2(r):
+        fin = {}
+
+        def post2_mult(r, i):
             cols = slice(256 * (r - 8), 256 * (r - 8) + 256)
             tiles = acc[r]
-            tmp = tmpp.tile([P, NB, 256], F32, name="tmp", tag="tmp")
-            ot = outp.tile([P, NB, 256], F32, name="ot", tag="ot")
+            if i == 0:
+                tmp = tmpp.tile([P, NB, 256], F32, name="tmp", tag="tmp")
+                ot = outp.tile([P, NB, 256], F32, name="ot", tag="ot")
+                fin[r] = (tmp, ot)
+            tmp, ot = fin[r]
             n = NB // len(tiles)
-            if r == ROUNDS - 1 and FINE_TAIL:
-                for b in range(NB + 1):
-                    if b < NB:
-                        nc.vector.tensor_tensor(out=tmp[:, b, :], in0=tiles[b][:, 0:256], in1=sc4b[:, cols], op=ALU.mult)
-                    if b >= 1:
-                        nc.vector.tensor_tensor(out=ot[:, b - 1, :], in0=tmp[:, b - 1, :], in1=biasb[:, cols], op=ALU.add)
-                        nc.sync.dma_start(out=out[b - 1][:, cols], in_=ot[:, b - 1, :])
-                return
-            for i, ps in enumerate(tiles):
-                nc.vector.tensor_tensor(
-                    out=tmp[:, n * i : n * i + n, :],
-                    in0=ps[:, 0 : 256 * n].rearrange("p (b o) -> p b o", b=n),
-                    in1=sc4b[:, cols].unsqueeze(1).to_broadcast([P, n, 256]),
-                    op=ALU.mult,
-                )
-            for h in range(2):
-                nc.vector.tensor_tensor(
-                    out=ot[:, 2 * h : 2 * h + 2, :],
-                    in0=tmp[:, 2 * h : 2 * h + 2, :],
-                    in1=biasb[:, cols].unsqueeze(1).to_broadcast([P, 2, 256]),
-                    op=ALU.add,
-                )
-            nc.sync.dma_start(out=out_v[:, :, cols], in_=ot[:])
+            nc.vector.tensor_tensor(
+                out=tmp[:, n * i : n * i + n, :],
+                in0=tiles[i][:, 0 : 256 * n].rearrange("p (b o) -> p b o", b=n),
+                in1=sc4b[:, cols].unsqueeze(1).to_broadcast([P, n, 256]),
+                op=ALU.mult,
+            )
+
+        def post2_add(r, b0, n, store):
+            cols = slice(256 * (r - 8), 256 * (r - 8) + 256)
+            tmp, ot = fin[r]
+            add_eng = nc.gpsimd if r >= POOL_ADD_FROM else nc.vector
+            add_eng.tensor_tensor(
+                out=ot[:, b0 : b0 + n, :],
+                in0=tmp[:, b0 : b0 + n, :],
+                in1=biasb[:, cols].unsqueeze(1).to_broadcast([P, n, 256]),
+                op=ALU.add,
+            )
+            if store:
+                nc.sync.dma_start(out=out_v[:, store[0] : store[1], cols], in_=ot[:, store[0] : store[1], :])
 
         transposes(0, "ssss")
-        quant_x(NB - 1)
-        quantise(0)
+        quant_x(1)
+        quantise(0, 0)
+        quantise(0, 1)
         for r in range(ROUNDS):
-            if r + 1 < ROUNDS:
+            nxt = r + 1 < ROUNDS
+            if nxt:
                 transposes(r + 1, B_ENG if r + 1 < 8 else A_ENG)
             if r < 8:
                 mx1(r)
-            else:
-                mx2(r)
-            if r + 1 < ROUNDS:
-                quantise(r + 1)
-            if r < 8:
+                quantise(r + 1, 0)
+                quantise(r + 1, 1)
                 post1(r)
             else:
-                post2(r)
+                mx2(r)
+                if len(acc[r]) == 2:
+                    if nxt:
+                        quantise(r + 1, 0)
+                    post2_mult(r, 0)
+                    if nxt:
+                        quantise(r + 1, 1)
+                    post2_mult(r, 1)
+                    post2_add(r, 0, 2, None)
+                    post2_add(r, 2, 2, (0, NB))
+                elif nxt:
+                    quantise(r + 1, 0)
+                    quantise(r + 1, 1)
+                    for i in range(NB):
+                        post2_mult(r, i)
+                    post2_add(r, 0, 2, None)
+                    post2_add(r, 2, 2, (0, NB))
+                else:
+                    for b in range(NB + 1):
+                        if b < NB:
+                            post2_mult(r, b)
+                        if b >= 1:
+                            post2_add(r, b - 1, 1, (b - 1, b))

@@ -17,18 +17,13 @@ D = 2048
 NB = 4
 G = 4
 ROUNDS = 16
-RAW_BUFS = 10
+RAW_BUFS = 9
 FLOPS = 2 * 512 * 2048 * 2048 * 2
 
-MULTS_FIRST = True
-FINE_TAIL = True
-A_BY_HALVES = True
-W0_HALVES = True
-ACT_PRELOAD = True
-SC2_LATE = True
-QX_PAIRS = True
-BC_SBUF = False
-POOL_ADD_FROM = 16
+N_WARM = 16
+GRP_BUFS = 4
+COD_BUFS = 4
+GROUPS = [[0], [1], [2], [3], [4, 5], [6, 7], [8, 9], [10, 11], [12, 13], [14, 15]]
 B_ENG = "sssv"
 A_ENG = "ssss"
 
@@ -38,35 +33,39 @@ def tile_doublebinarylinear_kernel(tc, x, scaling0, B, scaling2, A, scaling4, bi
     with ExitStack() as ctx:
         const = ctx.enter_context(tc.tile_pool(name="const", bufs=1))
         rawp = ctx.enter_context(tc.tile_pool(name="raw", bufs=RAW_BUFS))
-        grpp = ctx.enter_context(tc.tile_pool(name="grp", bufs=3))
-        codp = ctx.enter_context(tc.tile_pool(name="cod", bufs=3))
+        grpp = ctx.enter_context(tc.tile_pool(name="grp", bufs=GRP_BUFS))
+        codp = ctx.enter_context(tc.tile_pool(name="cod", bufs=COD_BUFS))
         h2p = ctx.enter_context(tc.tile_pool(name="h2", bufs=2))
         tmpp = ctx.enter_context(tc.tile_pool(name="tmpp", bufs=2))
         outp = ctx.enter_context(tc.tile_pool(name="outp", bufs=3))
-        tpp = ctx.enter_context(tc.psum_pool(name="tpp", bufs=4))
-        mmp = ctx.enter_context(tc.psum_pool(name="mmp", bufs=4))
+        psp = ctx.enter_context(tc.psum_pool(name="psp", bufs=8))
         ctx.enter_context(tc.manual_schedule())
 
-        a_pat = "(c e p) k -> c p e k" if A_BY_HALVES else "(c p e) k -> c p e k"
-        w_dram = [B.rearrange("(c p e) k -> c p e k", p=P, e=2), A.rearrange(a_pat, p=P, e=2)]
+        w_dram = [B.rearrange("(c p e) k -> c p e k", p=P, e=2), A.rearrange("(c e p) k -> c p e k", p=P, e=2)]
         out_v = out.rearrange("b s o -> s b o")
-
-        row0 = const.tile([P, D], BF16, name="row0")
-        nc.vector.memset(row0[:].bitcast(I32), 0)
-        nc.sync.dma_start(out=row0[0:1, :], in_=scaling0.rearrange("(o k) -> o k", o=1))
-        ones = const.tile([P, P], BF16, name="ones")
-        nc.vector.memset(ones[:], 1.0)
-        ident = const.tile([P, P], F32, name="ident")
-        make_identity(nc, ident[:])
-        if ACT_PRELOAD:
-            warm = const.tile([P, 1], BF16, name="warm")
-            nc.scalar.copy(out=warm[:], in_=ones[:, 0:1])
 
         x_sb = []
         for b in range(NB):
             xt = const.tile([P, D], BF16, name="x%d" % b)
-            nc.sync.dma_start(out=xt[:], in_=x[b])
             x_sb.append(xt)
+        nc.sync.dma_start(out=x_sb[0][:], in_=x[0])
+        s0_row = scaling0.rearrange("(o k) -> o k", o=1)
+        row0 = []
+        ones = const.tile([P, P], BF16, name="ones")
+        for h in range(2):
+            rt = const.tile([P, 1024], BF16, name="row0_%d" % h)
+            nc.vector.memset(rt[:].bitcast(I32), 0)
+            nc.sync.dma_start(out=rt[0:1, :], in_=s0_row[:, 1024 * h : 1024 * h + 1024])
+            row0.append(rt)
+            if h == 0:
+                nc.vector.memset(ones[:], 1.0)
+        ident = const.tile([P, P], F32, name="ident")
+        make_identity(nc, ident[:])
+        warm = const.tile([P, 1], BF16, name="warm")
+        nc.scalar.copy(out=warm[:], in_=ones[:, 0:1])
+
+        for b in range(1, NB):
+            nc.sync.dma_start(out=x_sb[b][:], in_=x[b])
         sc2raw = const.tile([P, 16], BF16, name="sc2raw")
         sc2t = const.tile([P, 16], F32, name="sc2t")
         sc4b = const.tile([P, D], BF16, name="sc4b")
@@ -76,7 +75,7 @@ def tile_doublebinarylinear_kernel(tc, x, scaling0, B, scaling2, A, scaling4, bi
 
         def load_w(r):
             w = rawp.tile([P, 2, D], BF16, name="w", tag="w")
-            if r == 0 and W0_HALVES:
+            if r == 0:
                 for e in range(2):
                     nc.sync.dma_start(out=w[:, e, :], in_=w_dram[0][0][:, e, :])
             else:
@@ -101,23 +100,22 @@ def tile_doublebinarylinear_kernel(tc, x, scaling0, B, scaling2, A, scaling4, bi
         h2q = const.tile([P, G * 512], U32, name="h2q", align_bytes=64)
         h2s = const.tile([P, G * 512], U8, name="h2s", align_bytes=64)
 
+        if N_WARM:
+            wt = psp.tile([P, 512], F32, name="ps", tag="ps")
+            for i in range(N_WARM):
+                nc.tensor.matmul(out=wt[:, 0:128], lhsT=ones[:], rhs=ones[:], start=True, stop=True)
         bc = []
         for h in range(2):
-            bt = mmp.tile([P, 1024], BF16, name="bc%d" % h, tag="mm")
+            bt = psp.tile([P, 1024], BF16, name="bc%d" % h, tag="ps")
             for q in range(2):
                 nc.tensor.matmul(
                     out=bt[:, 512 * q : 512 * q + 512],
                     lhsT=ones[:],
-                    rhs=row0[:, 1024 * h + 512 * q : 1024 * h + 512 * q + 512],
+                    rhs=row0[h][:, 512 * q : 512 * q + 512],
                     start=True,
                     stop=True,
                 )
-            if BC_SBUF:
-                bs = const.tile([P, 1024], BF16, name="bcs%d" % h)
-                nc.scalar.copy(out=bs[:], in_=bt[:])
-                bc.append(bs)
-            else:
-                bc.append(bt)
+            bc.append(bt)
 
         xg_f = xg[:].bitcast(F32).rearrange("p (g t u) -> p g t u", g=G, u=2)
 
@@ -135,7 +133,7 @@ def tile_doublebinarylinear_kernel(tc, x, scaling0, B, scaling2, A, scaling4, bi
             for j in range(2):
                 cols = slice(1024 * j, 1024 * j + 1024)
                 nc.vector.tensor_tensor(out=x_sb[b][:, cols], in0=x_sb[b][:, cols], in1=bc[j][:], op=ALU.mult)
-                t = tpp.tile([P, 512], F32, name="tp", tag="tp")
+                t = psp.tile([P, 512], F32, name="ps", tag="ps")
                 for a in range(2):
                     for u in range(2):
                         k0 = 256 * (2 * j + a) + 128 * u
@@ -160,7 +158,7 @@ def tile_doublebinarylinear_kernel(tc, x, scaling0, B, scaling2, A, scaling4, bi
             gt = grpp.tile([P, 4096], BF16, name="grp", tag="grp", align_bytes=64)
             gf = gt[:].bitcast(F32)
             for k in range(4):
-                t = tpp.tile([P, 512], F32, name="tp", tag="tp")
+                t = psp.tile([P, 512], F32, name="ps", tag="ps")
                 for a in range(2):
                     for u in range(2):
                         if r < 8:
@@ -173,12 +171,8 @@ def tile_doublebinarylinear_kernel(tc, x, scaling0, B, scaling2, A, scaling4, bi
                             in_=wf[:, e, k0 : k0 + 128],
                             identity=ident[:],
                         )
-                if r < 8 or A_BY_HALVES:
-                    dst = gf[:, 512 * k : 512 * k + 512].rearrange("p (a m u) -> p a m u", a=2, u=2)
-                    src = t[:].rearrange("p (a u m) -> p a m u", a=2, u=2)
-                else:
-                    dst = gf[:, 512 * k : 512 * k + 512].rearrange("p (m a u) -> p m a u", a=2, u=2)
-                    src = t[:].rearrange("p (a u m) -> p m a u", a=2, u=2)
+                dst = gf[:, 512 * k : 512 * k + 512].rearrange("p (a m u) -> p a m u", a=2, u=2)
+                src = t[:].rearrange("p (a u m) -> p a m u", a=2, u=2)
                 if engines[k] == "s":
                     nc.scalar.copy(out=dst, in_=src)
                 else:
@@ -206,7 +200,7 @@ def tile_doublebinarylinear_kernel(tc, x, scaling0, B, scaling2, A, scaling4, bi
         def mx1(c):
             wq, ws = cod[c]
             for e in range(2):
-                ps = mmp.tile([P, 512], F32, name="mm", tag="mm")
+                ps = psp.tile([P, 512], F32, name="ps", tag="ps")
                 for g in range(G):
                     c0 = e * 512 + g * 128
                     nc.tensor.matmul_mx(
@@ -265,16 +259,16 @@ def tile_doublebinarylinear_kernel(tc, x, scaling0, B, scaling2, A, scaling4, bi
             if r == 8:
                 tiles = []
                 for b in range(NB):
-                    ps = mmp.tile([P, 512], F32, name="mm", tag="mm")
+                    ps = psp.tile([P, 512], F32, name="ps", tag="ps")
                     tiles.append(ps)
                 for g in range(G):
                     for b in range(NB):
                         mx2_pass(tiles[b][:, 0:256], cd, b, g)
                 acc[r] = tiles
-            elif r == ROUNDS - 1 and FINE_TAIL:
+            elif r == ROUNDS - 1:
                 tiles = []
                 for b in range(NB):
-                    ps = mmp.tile([P, 512], F32, name="mm", tag="mm")
+                    ps = psp.tile([P, 512], F32, name="ps", tag="ps")
                     for g in range(G):
                         mx2_pass(ps[:, 0:256], cd, b, g)
                     tiles.append(ps)
@@ -282,7 +276,7 @@ def tile_doublebinarylinear_kernel(tc, x, scaling0, B, scaling2, A, scaling4, bi
             else:
                 tiles = []
                 for h in range(2):
-                    ps = mmp.tile([P, 512], F32, name="mm", tag="mm")
+                    ps = psp.tile([P, 512], F32, name="ps", tag="ps")
                     for bl in range(2):
                         for g in range(G):
                             mx2_pass(ps[:, 256 * bl : 256 * bl + 256], cd, 2 * h + bl, g)
@@ -310,8 +304,7 @@ def tile_doublebinarylinear_kernel(tc, x, scaling0, B, scaling2, A, scaling4, bi
         def post2_add(r, b0, n, store):
             cols = slice(256 * (r - 8), 256 * (r - 8) + 256)
             tmp, ot = fin[r]
-            add_eng = nc.gpsimd if r >= POOL_ADD_FROM else nc.vector
-            add_eng.tensor_tensor(
+            nc.vector.tensor_tensor(
                 out=ot[:, b0 : b0 + n, :],
                 in0=tmp[:, b0 : b0 + n, :],
                 in1=biasb[:, cols].unsqueeze(1).to_broadcast([P, n, 256]),
@@ -320,40 +313,50 @@ def tile_doublebinarylinear_kernel(tc, x, scaling0, B, scaling2, A, scaling4, bi
             if store:
                 nc.sync.dma_start(out=out_v[:, store[0] : store[1], cols], in_=ot[:, store[0] : store[1], :])
 
+        def post2_steps(r):
+            n_tiles = len(acc[r])
+            if r == ROUNDS - 1:
+                steps = []
+                for b in range(NB + 1):
+                    if b < NB:
+                        steps.append(("m", r, b))
+                    if b >= 1:
+                        steps.append(("a", r, b - 1, 1, (b - 1, b)))
+                return steps
+            steps = [("m", r, i) for i in range(n_tiles)]
+            steps.append(("a", r, 0, 2, None))
+            steps.append(("a", r, 2, 2, (0, NB)))
+            return steps
+
+        def run_step(s):
+            if s[0] == "m":
+                post2_mult(s[1], s[2])
+            elif s[0] == "a":
+                post2_add(s[1], s[2], s[3], s[4])
+            else:
+                quantise(s[1], s[2])
+
         transposes(0, "ssss")
         quant_x(1)
         quantise(0, 0)
         quantise(0, 1)
-        for r in range(ROUNDS):
-            nxt = r + 1 < ROUNDS
-            if nxt:
-                transposes(r + 1, B_ENG if r + 1 < 8 else A_ENG)
-            if r < 8:
-                mx1(r)
-                quantise(r + 1, 0)
-                quantise(r + 1, 1)
-                post1(r)
-            else:
-                mx2(r)
-                if len(acc[r]) == 2:
-                    if nxt:
-                        quantise(r + 1, 0)
-                    post2_mult(r, 0)
-                    if nxt:
-                        quantise(r + 1, 1)
-                    post2_mult(r, 1)
-                    post2_add(r, 0, 2, None)
-                    post2_add(r, 2, 2, (0, NB))
-                elif nxt:
-                    quantise(r + 1, 0)
-                    quantise(r + 1, 1)
-                    for i in range(NB):
-                        post2_mult(r, i)
-                    post2_add(r, 0, 2, None)
-                    post2_add(r, 2, 2, (0, NB))
+        for i, rounds in enumerate(GROUPS):
+            ahead = GROUPS[i + 1] if i + 1 < len(GROUPS) else []
+            for q in ahead:
+                transposes(q, B_ENG if q < 8 else A_ENG)
+            for r in rounds:
+                if r < 8:
+                    mx1(r)
                 else:
-                    for b in range(NB + 1):
-                        if b < NB:
-                            post2_mult(r, b)
-                        if b >= 1:
-                            post2_add(r, b - 1, 1, (b - 1, b))
+                    mx2(r)
+            quants = [("q", q, h) for q in ahead for h in range(2)]
+            if rounds[0] < 8:
+                for s in quants:
+                    run_step(s)
+                for r in rounds:
+                    post1(r)
+            else:
+                posts = [s for r in rounds for s in post2_steps(r)]
+                lead = len(quants) - 1 if (quants and len(acc[rounds[0]]) == 2) else len(quants)
+                for s in quants[:lead] + posts[:1] + quants[lead:] + posts[1:]:
+                    run_step(s)

@@ -24,6 +24,7 @@ N_WARM = 16
 GRP_BUFS = 4
 COD_BUFS = 4
 GROUPS = [[0], [1], [2], [3], [4, 5], [6, 7], [8, 9], [10, 11], [12, 13], [14, 15]]
+ROWS_BEHIND = [10, 15]
 B_ENG = "sssv"
 A_ENG = "ssss"
 
@@ -73,6 +74,11 @@ def tile_doublebinarylinear_kernel(tc, x, scaling0, B, scaling2, A, scaling4, bi
 
         raw = {}
 
+        def load_rows(h):
+            cols = slice(1024 * h, 1024 * h + 1024)
+            nc.sync.dma_start(out=sc4b[:, cols], in_=scaling4[cols].partition_broadcast(P))
+            nc.sync.dma_start(out=biasb[:, cols], in_=bias[cols].partition_broadcast(P))
+
         def load_w(r):
             w = rawp.tile([P, 2, D], BF16, name="w", tag="w")
             if r == 0:
@@ -81,6 +87,8 @@ def tile_doublebinarylinear_kernel(tc, x, scaling0, B, scaling2, A, scaling4, bi
             else:
                 nc.sync.dma_start(out=w[:], in_=w_dram[r // 8][r % 8])
             raw[r] = w
+            if r in ROWS_BEHIND:
+                load_rows(ROWS_BEHIND.index(r))
 
         for r in range(RAW_BUFS):
             load_w(r)
@@ -90,9 +98,6 @@ def tile_doublebinarylinear_kernel(tc, x, scaling0, B, scaling2, A, scaling4, bi
                         out=sc2raw[:].rearrange("p (c e) -> p c e", e=2),
                         in_=scaling2.rearrange("(c p e) -> p c e", p=P, e=2),
                     )
-            if r == 7:
-                nc.sync.dma_start(out=sc4b[:], in_=scaling4.partition_broadcast(P))
-                nc.sync.dma_start(out=biasb[:], in_=bias.partition_broadcast(P))
 
         xg = const.tile([P, G * 512 * 4], BF16, name="xg", align_bytes=64)
         xq = const.tile([P, G * 512], U32, name="xq", align_bytes=64)

@@ -67,7 +67,9 @@ def tile_doublebinarylinear_kernel(tc, x, scaling0, B, scaling2, A, scaling4, bi
 
         for b in range(1, NB):
             nc.sync.dma_start(out=x_sb[b][:], in_=x[b])
-        sc2raw = const.tile([P, 16], BF16, name="sc2raw")
+        s2w = const.tile([P, P], F32, name="s2w")
+        nc.gpsimd.memset(s2w[:], 0.0)
+        nc.sync.dma_start(out=s2w[0:8, :], in_=scaling2.bitcast(F32).rearrange("(c p) -> c p", p=P))
         sc2t = const.tile([P, 16], F32, name="sc2t")
         sc4b = const.tile([P, D], BF16, name="sc4b")
         biasb = const.tile([P, D], BF16, name="biasb")
@@ -92,12 +94,6 @@ def tile_doublebinarylinear_kernel(tc, x, scaling0, B, scaling2, A, scaling4, bi
 
         for r in range(RAW_BUFS):
             load_w(r)
-            if r == 0:
-                with nc.allow_non_contiguous_dma(reason="one small vector, two elements to a piece"):
-                    nc.sync.dma_start(
-                        out=sc2raw[:].rearrange("p (c e) -> p c e", e=2),
-                        in_=scaling2.rearrange("(c p e) -> p c e", p=P, e=2),
-                    )
 
         xg = const.tile([P, G * 512 * 4], BF16, name="xg", align_bytes=64)
         xq = const.tile([P, G * 512], U32, name="xq", align_bytes=64)
@@ -120,7 +116,9 @@ def tile_doublebinarylinear_kernel(tc, x, scaling0, B, scaling2, A, scaling4, bi
                     start=True,
                     stop=True,
                 )
-            bc.append(bt)
+            bs = const.tile([P, 1024], BF16, name="bcs%d" % h)
+            nc.scalar.copy(out=bs[:], in_=bt[:])
+            bc.append(bs)
 
         xg_f = xg[:].bitcast(F32).rearrange("p (g t u) -> p g t u", g=G, u=2)
 
@@ -151,7 +149,9 @@ def tile_doublebinarylinear_kernel(tc, x, scaling0, B, scaling2, A, scaling4, bi
                     out=xg_f[:, 2 * j : 2 * j + 2, 128 * b : 128 * b + 128, :],
                     in_=t[:].rearrange("p (a u m) -> p a m u", a=2, u=2),
                 )
-        nc.gpsimd.tensor_copy(out=sc2t[:], in_=sc2raw[:])
+        pv = psp.tile([P, 512], F32, name="ps", tag="ps")
+        nc.tensor.transpose(out=pv[:, 0:P], in_=s2w[:], identity=ident[:])
+        nc.scalar.copy(out=sc2t[:], in_=pv[:, 0:8].bitcast(BF16))
         quant_x(0)
 
         grp = {}

@@ -116,9 +116,7 @@ def tile_doublebinarylinear_kernel(tc, x, scaling0, B, scaling2, A, scaling4, bi
                     start=True,
                     stop=True,
                 )
-            bs = const.tile([P, 1024], BF16, name="bcs%d" % h)
-            nc.scalar.copy(out=bs[:], in_=bt[:])
-            bc.append(bs)
+            bc.append(bt)
 
         xg_f = xg[:].bitcast(F32).rearrange("p (g t u) -> p g t u", g=G, u=2)
 

@@ -23,7 +23,7 @@ FLOPS = 2 * 512 * 2048 * 2048 * 2
 N_WARM = 16
 GRP_BUFS = 4
 COD_BUFS = 4
-GROUPS = [[0], [1], [2], [3], [4, 5], [6, 7], [8, 9], [10, 11], [12, 13], [14, 15]]
+GROUPS = [[0], [1], [2, 3], [4, 5], [6, 7], [8, 9], [10, 11], [12], [13], [14], [15]]
 ROWS_BEHIND = [10, 15]
 B_ENG = "sssv"
 A_ENG = "ssss"

from contextlib import ExitStack

import concourse.mybir as mybir
from concourse.masks import make_identity

F32 = mybir.dt.float32
BF16 = mybir.dt.bfloat16
U32 = mybir.dt.uint32
U8 = mybir.dt.uint8
I32 = mybir.dt.int32
FP8X4 = mybir.dt.float8_e4m3fn_x4
ACT = mybir.ActivationFunctionType
ALU = mybir.AluOpType

P = 128
D = 2048
NB = 4
G = 4
ROUNDS = 16
RAW_BUFS = 9
FLOPS = 2 * 512 * 2048 * 2048 * 2

N_WARM = 16
GRP_BUFS = 4
COD_BUFS = 4
GROUPS = [[0], [1], [2, 3], [4, 5], [6, 7], [8, 9], [10, 11], [12], [13], [14], [15]]
ROWS_BEHIND = [10, 15]
B_ENG = "sssv"
A_ENG = "ssss"


def tile_doublebinarylinear_kernel(tc, x, scaling0, B, scaling2, A, scaling4, bias, out):
    nc = tc.nc
    with ExitStack() as ctx:
        const = ctx.enter_context(tc.tile_pool(name="const", bufs=1))
        rawp = ctx.enter_context(tc.tile_pool(name="raw", bufs=RAW_BUFS))
        grpp = ctx.enter_context(tc.tile_pool(name="grp", bufs=GRP_BUFS))
        codp = ctx.enter_context(tc.tile_pool(name="cod", bufs=COD_BUFS))
        h2p = ctx.enter_context(tc.tile_pool(name="h2", bufs=2))
        tmpp = ctx.enter_context(tc.tile_pool(name="tmpp", bufs=2))
        outp = ctx.enter_context(tc.tile_pool(name="outp", bufs=3))
        psp = ctx.enter_context(tc.psum_pool(name="psp", bufs=8))
        ctx.enter_context(tc.manual_schedule())

        w_dram = [B.rearrange("(c p e) k -> c p e k", p=P, e=2), A.rearrange("(c e p) k -> c p e k", p=P, e=2)]
        out_v = out.rearrange("b s o -> s b o")

        x_sb = []
        for b in range(NB):
            xt = const.tile([P, D], BF16, name="x%d" % b)
            x_sb.append(xt)
        nc.sync.dma_start(out=x_sb[0][:], in_=x[0])
        s0_row = scaling0.rearrange("(o k) -> o k", o=1)
        row0 = []
        ones = const.tile([P, P], BF16, name="ones")
        for h in range(2):
            rt = const.tile([P, 1024], BF16, name="row0_%d" % h)
            nc.vector.memset(rt[:].bitcast(I32), 0)
            nc.sync.dma_start(out=rt[0:1, :], in_=s0_row[:, 1024 * h : 1024 * h + 1024])
            row0.append(rt)
            if h == 0:
                nc.vector.memset(ones[:], 1.0)
        ident = const.tile([P, P], F32, name="ident")
        make_identity(nc, ident[:])
        warm = const.tile([P, 1], BF16, name="warm")
        nc.scalar.copy(out=warm[:], in_=ones[:, 0:1])

        for b in range(1, NB):
            nc.sync.dma_start(out=x_sb[b][:], in_=x[b])
        s2w = const.tile([P, P], F32, name="s2w")
        nc.gpsimd.memset(s2w[:], 0.0)
        nc.sync.dma_start(out=s2w[0:8, :], in_=scaling2.bitcast(F32).rearrange("(c p) -> c p", p=P))
        sc2t = const.tile([P, 16], F32, name="sc2t")
        sc4b = const.tile([P, D], BF16, name="sc4b")
        biasb = const.tile([P, D], BF16, name="biasb")

        raw = {}

        def load_rows(h):
            cols = slice(1024 * h, 1024 * h + 1024)
            nc.sync.dma_start(out=sc4b[:, cols], in_=scaling4[cols].partition_broadcast(P))
            nc.sync.dma_start(out=biasb[:, cols], in_=bias[cols].partition_broadcast(P))

        def load_w(r):
            w = rawp.tile([P, 2, D], BF16, name="w", tag="w")
            if r == 0:
                for e in range(2):
                    nc.sync.dma_start(out=w[:, e, :], in_=w_dram[0][0][:, e, :])
            else:
                nc.sync.dma_start(out=w[:], in_=w_dram[r // 8][r % 8])
            raw[r] = w
            if r in ROWS_BEHIND:
                load_rows(ROWS_BEHIND.index(r))

        for r in range(RAW_BUFS):
            load_w(r)

        xg = const.tile([P, G * 512 * 4], BF16, name="xg", align_bytes=64)
        xq = const.tile([P, G * 512], U32, name="xq", align_bytes=64)
        xsc = const.tile([P, G * 512], U8, name="xsc", align_bytes=64)
        h2q = const.tile([P, G * 512], U32, name="h2q", align_bytes=64)
        h2s = const.tile([P, G * 512], U8, name="h2s", align_bytes=64)

        if N_WARM:
            wt = psp.tile([P, 512], F32, name="ps", tag="ps")
            for i in range(N_WARM):
                nc.tensor.matmul(out=wt[:, 0:128], lhsT=ones[:], rhs=ones[:], start=True, stop=True)
        bc = []
        for h in range(2):
            bt = psp.tile([P, 1024], BF16, name="bc%d" % h, tag="ps")
            for q in range(2):
                nc.tensor.matmul(
                    out=bt[:, 512 * q : 512 * q + 512],
                    lhsT=ones[:],
                    rhs=row0[h][:, 512 * q : 512 * q + 512],
                    start=True,
                    stop=True,
                )
            bc.append(bt)

        xg_f = xg[:].bitcast(F32).rearrange("p (g t u) -> p g t u", g=G, u=2)

        def quant_x(bp):
            for g in range(G):
                c0 = g * 512 + 256 * bp
                nc.vector.quantize_mx(
                    out=xq[:, c0 : c0 + 256].bitcast(FP8X4),
                    scales=xsc[:, c0 : c0 + 256],
                    in_=xg[:, 4 * c0 : 4 * c0 + 1024],
                )

        for b in range(NB):
            xf = x_sb[b][:].bitcast(F32)
            for j in range(2):
                cols = slice(1024 * j, 1024 * j + 1024)
                nc.vector.tensor_tensor(out=x_sb[b][:, cols], in0=x_sb[b][:, cols], in1=bc[j][:], op=ALU.mult)
                t = psp.tile([P, 512], F32, name="ps", tag="ps")
                for a in range(2):
                    for u in range(2):
                        k0 = 256 * (2 * j + a) + 128 * u
                        nc.tensor.transpose(
                            out=t[:, (2 * a + u) * 128 : (2 * a + u) * 128 + 128],
                            in_=xf[:, k0 : k0 + 128],
                            identity=ident[:],
                        )
                nc.scalar.copy(
                    out=xg_f[:, 2 * j : 2 * j + 2, 128 * b : 128 * b + 128, :],
                    in_=t[:].rearrange("p (a u m) -> p a m u", a=2, u=2),
                )
        pv = psp.tile([P, 512], F32, name="ps", tag="ps")
        nc.tensor.transpose(out=pv[:, 0:P], in_=s2w[:], identity=ident[:])
        nc.scalar.copy(out=sc2t[:], in_=pv[:, 0:8].bitcast(BF16))
        quant_x(0)

        grp = {}
        cod = {}

        def transposes(r, engines):
            w = raw[r]
            wf = w[:].bitcast(F32)
            gt = grpp.tile([P, 4096], BF16, name="grp", tag="grp", align_bytes=64)
            gf = gt[:].bitcast(F32)
            for k in range(4):
                t = psp.tile([P, 512], F32, name="ps", tag="ps")
                for a in range(2):
                    for u in range(2):
                        if r < 8:
                            e, g = k // 2, 2 * (k % 2) + a
                        else:
                            e, g = a, k
                        k0 = 256 * g + 128 * u
                        nc.tensor.transpose(
                            out=t[:, (2 * a + u) * 128 : (2 * a + u) * 128 + 128],
                            in_=wf[:, e, k0 : k0 + 128],
                            identity=ident[:],
                        )
                dst = gf[:, 512 * k : 512 * k + 512].rearrange("p (a m u) -> p a m u", a=2, u=2)
                src = t[:].rearrange("p (a u m) -> p a m u", a=2, u=2)
                if engines[k] == "s":
                    nc.scalar.copy(out=dst, in_=src)
                else:
                    nc.vector.tensor_copy(out=dst, in_=src)
            grp[r] = gt
            if r + RAW_BUFS < ROUNDS:
                load_w(r + RAW_BUFS)

        def quantise(r, h):
            gt = grp[r]
            if h == 0:
                wq = codp.tile([P, 1024], U32, name="wq", tag="wq", align_bytes=64)
                ws = codp.tile([P, 1024], U8, name="ws", tag="ws", align_bytes=64)
                cod[r] = (wq, ws)
            wq, ws = cod[r]
            nc.vector.quantize_mx(
                out=wq[:, 512 * h : 512 * h + 512].bitcast(FP8X4),
                scales=ws[:, 512 * h : 512 * h + 512],
                in_=gt[:, 2048 * h : 2048 * h + 2048],
            )

        acc = {}
        h2c = {}

        def mx1(c):
            wq, ws = cod[c]
            for e in range(2):
                ps = psp.tile([P, 512], F32, name="ps", tag="ps")
                for g in range(G):
                    c0 = e * 512 + g * 128
                    nc.tensor.matmul_mx(
                        out=ps[:],
                        lhsT=wq[:, c0 : c0 + 128].bitcast(FP8X4),
                        lhsT_scale=ws[:, c0 : c0 + 128],
                        rhs=xq[:, g * 512 : g * 512 + 512].bitcast(FP8X4),
                        rhs_scale=xsc[:, g * 512 : g * 512 + 512],
                        start=(g == 0),
                        stop=(g == G - 1),
                    )
                acc[(c, e)] = ps

        def post1(c):
            if c % 2 == 0:
                h2c[c // 2] = h2p.tile([P, 4, 512], BF16, name="h2c", tag="h2c")
            hc = h2c[c // 2]
            for e in range(2):
                nc.scalar.activation(
                    out=hc[:, 2 * (c % 2) + e, :],
                    in_=acc[(c, e)][:],
                    func=ACT.Copy,
                    scale=sc2t[:, 2 * c + e : 2 * c + e + 1],
                )
            if c % 2 == 1:
                g2 = c // 2
                hg = h2p.tile([P, 2048], BF16, name="h2g", tag="h2g", align_bytes=64)
                for h in range(2):
                    nc.vector.tensor_copy(
                        out=hg[:, 1024 * h : 1024 * h + 1024].rearrange("p (c i t) -> p c t i", i=4, t=4),
                        in_=hc[:, :, 256 * h : 256 * h + 256].rearrange("p t (c i) -> p c t i", i=4),
                    )
                for h in range(2):
                    c0 = g2 * 512 + 256 * h
                    nc.vector.quantize_mx(
                        out=h2q[:, c0 : c0 + 256].bitcast(FP8X4),
                        scales=h2s[:, c0 : c0 + 256],
                        in_=hg[:, 1024 * h : 1024 * h + 1024],
                    )

        def mx2_pass(ps_ap, cd, b, g):
            wq, ws = cd
            c0 = g * 512 + 128 * b
            nc.tensor.matmul_mx(
                out=ps_ap,
                lhsT=h2q[:, c0 : c0 + 128].bitcast(FP8X4),
                lhsT_scale=h2s[:, c0 : c0 + 128],
                rhs=wq[:, g * 256 : g * 256 + 256].bitcast(FP8X4),
                rhs_scale=ws[:, g * 256 : g * 256 + 256],
                start=(g == 0),
                stop=(g == G - 1),
            )

        def mx2(r):
            cd = cod[r]
            if r == 8:
                tiles = []
                for b in range(NB):
                    ps = psp.tile([P, 512], F32, name="ps", tag="ps")
                    tiles.append(ps)
                for g in range(G):
                    for b in range(NB):
                        mx2_pass(tiles[b][:, 0:256], cd, b, g)
                acc[r] = tiles
            elif r == ROUNDS - 1:
                tiles = []
                for b in range(NB):
                    ps = psp.tile([P, 512], F32, name="ps", tag="ps")
                    for g in range(G):
                        mx2_pass(ps[:, 0:256], cd, b, g)
                    tiles.append(ps)
                acc[r] = tiles
            else:
                tiles = []
                for h in range(2):
                    ps = psp.tile([P, 512], F32, name="ps", tag="ps")
                    for bl in range(2):
                        for g in range(G):
                            mx2_pass(ps[:, 256 * bl : 256 * bl + 256], cd, 2 * h + bl, g)
                    tiles.append(ps)
                acc[r] = tiles

        fin = {}

        def post2_mult(r, i):
            cols = slice(256 * (r - 8), 256 * (r - 8) + 256)
            tiles = acc[r]
            if i == 0:
                tmp = tmpp.tile([P, NB, 256], F32, name="tmp", tag="tmp")
                ot = outp.tile([P, NB, 256], F32, name="ot", tag="ot")
                fin[r] = (tmp, ot)
            tmp, ot = fin[r]
            n = NB // len(tiles)
            nc.vector.tensor_tensor(
                out=tmp[:, n * i : n * i + n, :],
                in0=tiles[i][:, 0 : 256 * n].rearrange("p (b o) -> p b o", b=n),
                in1=sc4b[:, cols].unsqueeze(1).to_broadcast([P, n, 256]),
                op=ALU.mult,
            )

        def post2_add(r, b0, n, store):
            cols = slice(256 * (r - 8), 256 * (r - 8) + 256)
            tmp, ot = fin[r]
            nc.vector.tensor_tensor(
                out=ot[:, b0 : b0 + n, :],
                in0=tmp[:, b0 : b0 + n, :],
                in1=biasb[:, cols].unsqueeze(1).to_broadcast([P, n, 256]),
                op=ALU.add,
            )
            if store:
                nc.sync.dma_start(out=out_v[:, store[0] : store[1], cols], in_=ot[:, store[0] : store[1], :])

        def post2_steps(r):
            n_tiles = len(acc[r])
            if r == ROUNDS - 1:
                steps = []
                for b in range(NB + 1):
                    if b < NB:
                        steps.append(("m", r, b))
                    if b >= 1:
                        steps.append(("a", r, b - 1, 1, (b - 1, b)))
                return steps
            steps = [("m", r, i) for i in range(n_tiles)]
            steps.append(("a", r, 0, 2, None))
            steps.append(("a", r, 2, 2, (0, NB)))
            return steps

        def run_step(s):
            if s[0] == "m":
                post2_mult(s[1], s[2])
            elif s[0] == "a":
                post2_add(s[1], s[2], s[3], s[4])
            else:
                quantise(s[1], s[2])

        transposes(0, "ssss")
        quant_x(1)
        quantise(0, 0)
        quantise(0, 1)
        for i, rounds in enumerate(GROUPS):
            ahead = GROUPS[i + 1] if i + 1 < len(GROUPS) else []
            for q in ahead:
                transposes(q, B_ENG if q < 8 else A_ENG)
            for r in rounds:
                if r < 8:
                    mx1(r)
                else:
                    mx2(r)
            quants = [("q", q, h) for q in ahead for h in range(2)]
            if rounds[0] < 8:
                for s in quants:
                    run_step(s)
                for r in rounds:
                    post1(r)
            else:
                posts = [s for r in rounds for s in post2_steps(r)]
                lead = len(quants) - 1 if (quants and len(acc[rounds[0]]) == 2) else len(quants)
                for s in quants[:lead] + posts[:1] + quants[lead:] + posts[1:]:
                    run_step(s)
